import numpy as np
import ml_dtypes


def mxq(x, axis, fmt="e4m3"):
    dtype, down = {"e4m3": (ml_dtypes.float8_e4m3fn, 7), "e5m2": (ml_dtypes.float8_e5m2, 14)}[fmt]
    v = np.moveaxis(np.asarray(x, np.float32).astype(ml_dtypes.bfloat16).astype(np.float64), axis, -1)
    blocks = v.reshape(v.shape[:-1] + (-1, 32))
    amax = np.abs(blocks).max(-1, keepdims=True)
    byte = np.maximum(np.where(amax > 0, np.frexp(amax)[1] - 1 + 127, 0) - down, 1)
    scale = np.exp2(byte - 127.0)
    codes = (blocks / scale).astype(np.float32).astype(dtype).astype(np.float64)
    return np.moveaxis((codes * scale).reshape(v.shape), -1, axis)


WIDE = False


def mx_kscale(k):
    if not WIDE:
        return np.ones(k)
    levels = np.array([20, -20, 10, -10, 0])
    a = np.random.permutation(np.resize(levels, k // 512 * 4)).reshape(k // 512, 4)
    idx = np.arange(k)
    return np.exp2(a[idx // 512, idx % 128 // 32])


BF16 = ml_dtypes.bfloat16


def bf(x):
    return np.asarray(x, np.float32).astype(BF16)


def f64(x):
    return np.asarray(x).astype(np.float64)


M, N, E, P, S, B, KT = 512, 512, 16, 32, 17, 512, 2


def gate(mlp_out, t2):
    lg = -f64(mlp_out).T / f64(t2)[0]
    ex = np.exp(lg - lg.max(axis=0, keepdims=True))
    return ex / ex.sum(axis=0, keepdims=True)


def relu_tail(z):
    return np.concatenate([z[:-P], np.maximum(z[-P:], 0.0)], axis=0)


def setup_inputs():
    s = mx_kscale(B)[None, :]
    z = np.random.standard_normal((M, B)) * s
    mlp_out = np.random.standard_normal((B, E)) * 0.65
    t2 = 0.5 + 0.1 * np.random.random_sample(1)
    A = np.random.standard_normal((E, M)) * 0.5
    W = np.random.standard_normal((E, M, M)) / np.sqrt(M)
    h = np.random.standard_normal((E, M)) * 0.1
    g = np.random.standard_normal((M, B)) * np.exp2(np.random.randint(-12, 1, (1, B))) * 8.0 / s
    return {"z": bf(z), "mlp_out": bf(mlp_out), "t2": bf(t2), "A": bf(A), "W": bf(W), "h": bf(h), "grad_out": bf(g)}


def reference(z, mlp_out, t2, A, W, h, grad_out):
    w_exp = gate(mlp_out, t2)
    zcat = relu_tail(f64(z))
    gw = f64(grad_out)[None, :, :] * w_exp[:, None, :]
    return mxq(gw, 2, "e5m2") @ mxq(zcat, 1, "e4m3").T

@@ -1,0 +1,160 @@
+from contextlib import ExitStack
+
+import concourse.mybir as mybir
+from concourse.masks import make_identity
+
+BF16 = mybir.dt.bfloat16
+F32 = mybir.dt.float32
+U32 = mybir.dt.uint32
+U8 = mybir.dt.uint8
+E5M2_X4 = mybir.dt.float8_e5m2_x4
+E4M3_X4 = mybir.dt.float8_e4m3fn_x4
+ALU = mybir.AluOpType
+X = mybir.AxisListType.X
+
+P = 128
+PACK = 4
+TOKENS = P * PACK
+EXPERTS = 16
+ROWS = 512
+COLS = 512
+RELU_ROWS = 32
+ROW_TILES = ROWS // P
+COL_TILES = COLS // P
+
+FLOPS = 2 * EXPERTS * ROWS * COLS * TOKENS
+BYTES = 2 * (ROWS * TOKENS + COLS * TOKENS + TOKENS * EXPERTS + 1) + 4 * EXPERTS * ROWS * COLS
+
+
+def tile_dynamix_pb_kernel(tc, z, mlp_out, t2, A, W, h, grad_out, out):
+    nc = tc.nc
+    with ExitStack() as ctx:
+        keep = ctx.enter_context(tc.tile_pool(name="keep", bufs=1))
+        work = ctx.enter_context(tc.tile_pool(name="work", bufs=3))
+        stage = ctx.enter_context(tc.tile_pool(name="stage", bufs=4))
+        turned = ctx.enter_context(tc.psum_pool(name="turned", bufs=2))
+        sums = ctx.enter_context(tc.psum_pool(name="sums", bufs=6))
+
+        logits = keep.tile([P, PACK, EXPERTS], BF16)
+        nc.sync.dma_start(out=logits[:], in_=mlp_out.rearrange("(t p) e -> p t e", p=P))
+        temperature = keep.tile([P, 1], BF16)
+        nc.sync.dma_start(out=temperature[:], in_=t2.partition_broadcast(P))
+        g_rows = keep.tile([P, ROW_TILES, TOKENS], BF16)
+        nc.sync.dma_start(out=g_rows[:], in_=grad_out.rearrange("(r i) b -> r i b", i=ROW_TILES))
+        z_rows = keep.tile([P, COL_TILES, TOKENS], BF16)
+        nc.sync.dma_start(out=z_rows[:], in_=z.rearrange("(i r) b -> r i b", r=P))
+
+        identity = keep.tile([P, P], BF16)
+        make_identity(nc, identity[:])
+
+        inv_t = keep.tile([P, 1], F32)
+        nc.vector.reciprocal(out=inv_t[:], in_=temperature[:])
+        scores = keep.tile([P, PACK, EXPERTS], F32)
+        nc.vector.tensor_scalar(
+            out=scores[:], in0=logits[:], scalar1=inv_t[:, 0:1], scalar2=-1.0, op0=ALU.mult, op1=ALU.mult
+        )
+        top = keep.tile([P, PACK], F32)
+        nc.vector.tensor_reduce(out=top[:], in_=scores[:], axis=X, op=ALU.max)
+        nc.vector.tensor_tensor(
+            out=scores[:],
+            in0=scores[:],
+            in1=top[:].unsqueeze(2).to_broadcast([P, PACK, EXPERTS]),
+            op=ALU.subtract,
+        )
+        powers = keep.tile([P, PACK, EXPERTS], F32)
+        nc.scalar.activation(out=powers[:], in_=scores[:], func=mybir.ActivationFunctionType.Exp)
+        total = keep.tile([P, PACK], F32)
+        nc.vector.tensor_reduce(out=total[:], in_=powers[:], axis=X, op=ALU.add)
+        inv_total = keep.tile([P, PACK], F32)
+        nc.vector.reciprocal(out=inv_total[:], in_=total[:])
+        gate = keep.tile([P, PACK, EXPERTS], F32)
+        nc.vector.tensor_tensor(
+            out=gate[:],
+            in0=powers[:],
+            in1=inv_total[:].unsqueeze(2).to_broadcast([P, PACK, EXPERTS]),
+            op=ALU.mult,
+        )
+
+        g_planes = keep.tile([P, PACK, ROWS], BF16)
+        for half in range(2):
+            g_turned = turned.tile([P, 2, ROWS], BF16, tag="turned")
+            for j in range(2):
+                t = 2 * half + j
+                for i in range(ROW_TILES):
+                    nc.tensor.transpose(
+                        g_turned[:, j, i * P : (i + 1) * P], g_rows[:, i, t * P : (t + 1) * P], identity[:]
+                    )
+            copy = nc.vector.tensor_copy if half == 0 else nc.scalar.copy
+            copy(out=g_planes[:, 2 * half : 2 * half + 2, :], in_=g_turned[:])
+
+        z_grouped = keep.tile([P, COLS, PACK], BF16, align_bytes=64)
+        half_cols = COLS // 2
+        for half in range(2):
+            z_turned = turned.tile([P, PACK, half_cols], BF16, tag="turned")
+            for t in range(PACK):
+                for j in range(2):
+                    i = 2 * half + j
+                    nc.tensor.transpose(
+                        z_turned[:, t, j * P : (j + 1) * P], z_rows[:, i, t * P : (t + 1) * P], identity[:]
+                    )
+            nc.scalar.copy(
+                out=z_grouped[:, half * half_cols : (half + 1) * half_cols, :],
+                in_=z_turned[:].rearrange("p t k -> p k t"),
+            )
+        nc.vector.tensor_scalar_max(
+            out=z_grouped[:, COLS - RELU_ROWS :, :], in0=z_grouped[:, COLS - RELU_ROWS :, :], scalar1=0.0
+        )
+        z_codes = keep.tile([P, COLS], U32, align_bytes=64)
+        z_scales = keep.tile([P, COLS], U8, align_bytes=64)
+        nc.vector.quantize_mx(
+            out=z_codes[:].bitcast(E4M3_X4), scales=z_scales[:], in_=z_grouped[:].rearrange("p k t -> p (k t)")
+        )
+
+        def weigh(e):
+            planes = work.tile([P, PACK, ROWS], BF16, tag="planes")
+            for t in range(PACK):
+                nc.vector.tensor_scalar(
+                    out=planes[:, t, :], in0=g_planes[:, t, :], scalar1=gate[:, t, e : e + 1], scalar2=None,
+                    op0=ALU.mult,
+                )
+            return planes
+
+        def group(planes):
+            grouped = work.tile([P, ROWS, PACK], BF16, tag="grouped", align_bytes=64)
+            nc.vector.tensor_copy(
+                out=grouped[:].rearrange("p (c n) t -> p c t n", n=4),
+                in_=planes[:].rearrange("p t (c n) -> p c t n", n=4),
+            )
+            return grouped
+
+        def multiply(e, grouped):
+            codes = work.tile([P, ROWS], U32, tag="codes", align_bytes=64)
+            scales = work.tile([P, ROWS], U8, tag="scales", align_bytes=64)
+            nc.vector.quantize_mx(
+                out=codes[:].bitcast(E5M2_X4), scales=scales[:], in_=grouped[:].rearrange("p m t -> p (m t)")
+            )
+            result = stage.tile([P, ROW_TILES, COLS], F32, tag="result")
+            for i in range(ROW_TILES):
+                rows = slice(i * P, (i + 1) * P)
+                acc = sums.tile([P, COLS], F32, tag="acc")
+                nc.tensor.matmul_mx(
+                    out=acc[:],
+                    lhsT=codes[:, rows].bitcast(E5M2_X4),
+                    lhsT_scale=scales[:, rows],
+                    rhs=z_codes[:].bitcast(E4M3_X4),
+                    rhs_scale=z_scales[:],
+                    start=True,
+                    stop=True,
+                )
+                nc.scalar.copy(out=result[:, i, :], in_=acc[:])
+            nc.sync.dma_start(out=out[e].rearrange("(r i) k -> r i k", i=ROW_TILES), in_=result[:])
+
+        planes_of = {}
+        grouped_of = {}
+        for step in range(EXPERTS + 2):
+            if step < EXPERTS:
+                planes_of[step] = weigh(step)
+            if 1 <= step <= EXPERTS:
+                grouped_of[step - 1] = group(planes_of[step - 1])
+            if step >= 2:
+                multiply(step - 2, grouped_of[step - 2])

@@ -14,6 +14,7 @@ X = mybir.AxisListType.X
 
 P = 128
 PACK = 4
+PAIR = 2
 TOKENS = P * PACK
 EXPERTS = 16
 ROWS = 512
@@ -21,6 +22,7 @@ COLS = 512
 RELU_ROWS = 32
 ROW_TILES = ROWS // P
 COL_TILES = COLS // P
+BANKS_PER_STORE = 2
 
 FLOPS = 2 * EXPERTS * ROWS * COLS * TOKENS
 BYTES = 2 * (ROWS * TOKENS + COLS * TOKENS + TOKENS * EXPERTS + 1) + 4 * EXPERTS * ROWS * COLS
@@ -31,12 +33,15 @@ def tile_dynamix_pb_kernel(tc, z, mlp_out, t2, A, W, h, grad_out, out):
     with ExitStack() as ctx:
         keep = ctx.enter_context(tc.tile_pool(name="keep", bufs=1))
         work = ctx.enter_context(tc.tile_pool(name="work", bufs=3))
-        stage = ctx.enter_context(tc.tile_pool(name="stage", bufs=4))
+        stage = ctx.enter_context(tc.tile_pool(name="stage", bufs=8))
         turned = ctx.enter_context(tc.psum_pool(name="turned", bufs=2))
         sums = ctx.enter_context(tc.psum_pool(name="sums", bufs=6))
 
         logits = keep.tile([P, PACK, EXPERTS], BF16)
-        nc.sync.dma_start(out=logits[:], in_=mlp_out.rearrange("(t p) e -> p t e", p=P))
+        nc.sync.dma_start(
+            out=logits[:].rearrange("p (u c) e -> p u c e", c=PAIR),
+            in_=mlp_out.rearrange("(u p c) e -> p u c e", p=P, c=PAIR),
+        )
         temperature = keep.tile([P, 1], BF16)
         nc.sync.dma_start(out=temperature[:], in_=t2.partition_broadcast(P))
         g_rows = keep.tile([P, ROW_TILES, TOKENS], BF16)
@@ -44,7 +49,7 @@ def tile_dynamix_pb_kernel(tc, z, mlp_out, t2, A, W, h, grad_out, out):
         z_rows = keep.tile([P, COL_TILES, TOKENS], BF16)
         nc.sync.dma_start(out=z_rows[:], in_=z.rearrange("(i r) b -> r i b", r=P))
 
-        identity = keep.tile([P, P], BF16)
+        identity = keep.tile([P, P], F32)
         make_identity(nc, identity[:])
 
         inv_t = keep.tile([P, 1], F32)
@@ -76,39 +81,43 @@ def tile_dynamix_pb_kernel(tc, z, mlp_out, t2, A, W, h, grad_out, out):
         )
 
         g_planes = keep.tile([P, PACK, ROWS], BF16)
-        for half in range(2):
-            g_turned = turned.tile([P, 2, ROWS], BF16, tag="turned")
-            for j in range(2):
-                t = 2 * half + j
-                for i in range(ROW_TILES):
-                    nc.tensor.transpose(
-                        g_turned[:, j, i * P : (i + 1) * P], g_rows[:, i, t * P : (t + 1) * P], identity[:]
-                    )
-            copy = nc.vector.tensor_copy if half == 0 else nc.scalar.copy
-            copy(out=g_planes[:, 2 * half : 2 * half + 2, :], in_=g_turned[:])
+        for u in range(2):
+            g_turned = turned.tile([P, ROWS], F32, tag="turned")
+            for i in range(ROW_TILES):
+                nc.tensor.transpose(
+                    g_turned[:, i * P : (i + 1) * P],
+                    g_rows[:, i, :].bitcast(F32)[:, u * P : (u + 1) * P],
+                    identity[:],
+                )
+            copy = nc.vector.tensor_copy if u == 0 else nc.scalar.copy
+            copy(
+                out=g_planes[:, PAIR * u : PAIR * (u + 1), :],
+                in_=g_turned[:].bitcast(BF16).rearrange("p (m c) -> p c m", c=PAIR),
+            )
 
-        z_grouped = keep.tile([P, COLS, PACK], BF16, align_bytes=64)
+        z_pairs = keep.tile([P, COLS, 2], F32, align_bytes=64)
         half_cols = COLS // 2
         for half in range(2):
-            z_turned = turned.tile([P, PACK, half_cols], BF16, tag="turned")
-            for t in range(PACK):
+            z_turned = turned.tile([P, 2, half_cols], F32, tag="turned")
+            for u in range(2):
                 for j in range(2):
-                    i = 2 * half + j
                     nc.tensor.transpose(
-                        z_turned[:, t, j * P : (j + 1) * P], z_rows[:, i, t * P : (t + 1) * P], identity[:]
+                        z_turned[:, u, j * P : (j + 1) * P],
+                        z_rows[:, 2 * half + j, :].bitcast(F32)[:, u * P : (u + 1) * P],
+                        identity[:],
                     )
             nc.scalar.copy(
-                out=z_grouped[:, half * half_cols : (half + 1) * half_cols, :],
-                in_=z_turned[:].rearrange("p t k -> p k t"),
+                out=z_pairs[:, half * half_cols : (half + 1) * half_cols, :],
+                in_=z_turned[:].rearrange("p u k -> p k u"),
             )
-        nc.vector.tensor_scalar_max(
-            out=z_grouped[:, COLS - RELU_ROWS :, :], in0=z_grouped[:, COLS - RELU_ROWS :, :], scalar1=0.0
-        )
+        z_grouped = z_pairs[:].rearrange("p k u -> p (k u)").bitcast(BF16)
         z_codes = keep.tile([P, COLS], U32, align_bytes=64)
         z_scales = keep.tile([P, COLS], U8, align_bytes=64)
-        nc.vector.quantize_mx(
-            out=z_codes[:].bitcast(E4M3_X4), scales=z_scales[:], in_=z_grouped[:].rearrange("p k t -> p (k t)")
-        )
+
+        def quantise_z():
+            relu_part = z_grouped[:, (COLS - RELU_ROWS) * PACK :]
+            nc.vector.tensor_scalar_max(out=relu_part, in0=relu_part, scalar1=0.0)
+            nc.vector.quantize_mx(out=z_codes[:].bitcast(E4M3_X4), scales=z_scales[:], in_=z_grouped)
 
         def weigh(e):
             planes = work.tile([P, PACK, ROWS], BF16, tag="planes")
@@ -133,28 +142,30 @@ def tile_dynamix_pb_kernel(tc, z, mlp_out, t2, A, W, h, grad_out, out):
             nc.vector.quantize_mx(
                 out=codes[:].bitcast(E5M2_X4), scales=scales[:], in_=grouped[:].rearrange("p m t -> p (m t)")
             )
-            result = stage.tile([P, ROW_TILES, COLS], F32, tag="result")
-            for i in range(ROW_TILES):
-                rows = slice(i * P, (i + 1) * P)
-                acc = sums.tile([P, COLS], F32, tag="acc")
-                nc.tensor.matmul_mx(
-                    out=acc[:],
-                    lhsT=codes[:, rows].bitcast(E5M2_X4),
-                    lhsT_scale=scales[:, rows],
-                    rhs=z_codes[:].bitcast(E4M3_X4),
-                    rhs_scale=z_scales[:],
-                    start=True,
-                    stop=True,
-                )
-                nc.scalar.copy(out=result[:, i, :], in_=acc[:])
-            nc.sync.dma_start(out=out[e].rearrange("(r i) k -> r i k", i=ROW_TILES), in_=result[:])
+            out_rows = out[e].rearrange("(r i) k -> r i k", i=ROW_TILES)
+            for first in range(0, ROW_TILES, BANKS_PER_STORE):
+                result = stage.tile([P, BANKS_PER_STORE, COLS], F32, tag="result")
+                for j in range(BANKS_PER_STORE):
+                    rows = slice((first + j) * P, (first + j + 1) * P)
+                    acc = sums.tile([P, COLS], F32, tag="acc")
+                    nc.tensor.matmul_mx(
+                        out=acc[:],
+                        lhsT=codes[:, rows].bitcast(E5M2_X4),
+                        lhsT_scale=scales[:, rows],
+                        rhs=z_codes[:].bitcast(E4M3_X4),
+                        rhs_scale=z_scales[:],
+                        start=True,
+                        stop=True,
+                    )
+                    nc.scalar.copy(out=result[:, j, :], in_=acc[:])
+                nc.sync.dma_start(out=out_rows[:, first : first + BANKS_PER_STORE, :], in_=result[:])
 
-        planes_of = {}
-        grouped_of = {}
-        for step in range(EXPERTS + 2):
-            if step < EXPERTS:
-                planes_of[step] = weigh(step)
-            if 1 <= step <= EXPERTS:
-                grouped_of[step - 1] = group(planes_of[step - 1])
-            if step >= 2:
-                multiply(step - 2, grouped_of[step - 2])
+        grouped_now = group(weigh(0))
+        planes_next = weigh(1)
+        quantise_z()
+        for e in range(EXPERTS):
+            multiply(e, grouped_now)
+            if e + 1 < EXPERTS:
+                grouped_now = group(planes_next)
+            if e + 2 < EXPERTS:
+                planes_next = weigh(e + 2)

@@ -11,6 +11,7 @@ E5M2_X4 = mybir.dt.float8_e5m2_x4
 E4M3_X4 = mybir.dt.float8_e4m3fn_x4
 ALU = mybir.AluOpType
 X = mybir.AxisListType.X
+ACT = mybir.ActivationFunctionType
 
 P = 128
 PACK = 4
@@ -22,6 +23,7 @@ COLS = 512
 RELU_ROWS = 32
 ROW_TILES = ROWS // P
 COL_TILES = COLS // P
+HALF = 2 * P
 BANKS_PER_STORE = 2
 
 FLOPS = 2 * EXPERTS * ROWS * COLS * TOKENS
@@ -45,12 +47,26 @@ def tile_dynamix_pb_kernel(tc, z, mlp_out, t2, A, W, h, grad_out, out):
         temperature = keep.tile([P, 1], BF16)
         nc.sync.dma_start(out=temperature[:], in_=t2.partition_broadcast(P))
         g_rows = keep.tile([P, ROW_TILES, TOKENS], BF16)
-        nc.sync.dma_start(out=g_rows[:], in_=grad_out.rearrange("(r i) b -> r i b", i=ROW_TILES))
+        g_source = grad_out.rearrange("(r i) b -> r i b", i=ROW_TILES)
         z_rows = keep.tile([P, COL_TILES, TOKENS], BF16)
-        nc.sync.dma_start(out=z_rows[:], in_=z.rearrange("(i r) b -> r i b", r=P))
+        z_source = z.rearrange("(i r) b -> r i b", r=P)
+        for rows, source in ((g_rows, g_source), (z_rows, z_source)):
+            for half in range(2):
+                nc.sync.dma_start(out=rows[:, 2 * half : 2 * half + 2, :], in_=source[:, 2 * half : 2 * half + 2, :])
 
         identity = keep.tile([P, P], F32)
         make_identity(nc, identity[:])
+
+        def turn(rows, half):
+            pairs = turned.tile([P, 2, HALF], F32, tag="pairs")
+            for u in range(2):
+                for j in range(2):
+                    nc.tensor.transpose(
+                        pairs[:, u, j * P : (j + 1) * P],
+                        rows[:, 2 * half + j, :].bitcast(F32)[:, u * P : (u + 1) * P],
+                        identity[:],
+                    )
+            return pairs
 
         inv_t = keep.tile([P, 1], F32)
         nc.vector.reciprocal(out=inv_t[:], in_=temperature[:])
@@ -67,7 +83,17 @@ def tile_dynamix_pb_kernel(tc, z, mlp_out, t2, A, W, h, grad_out, out):
             op=ALU.subtract,
         )
         powers = keep.tile([P, PACK, EXPERTS], F32)
-        nc.scalar.activation(out=powers[:], in_=scores[:], func=mybir.ActivationFunctionType.Exp)
+        nc.scalar.activation(out=powers[:], in_=scores[:], func=ACT.Exp)
+
+        g_planes = keep.tile([P, PACK, ROWS], BF16)
+        for half in range(2):
+            pairs = turn(g_rows, half)
+            copy = nc.vector.tensor_copy if half == 0 else nc.scalar.copy
+            copy(
+                out=g_planes[:, :, half * HALF : (half + 1) * HALF].rearrange("p (u c) m -> p u c m", c=PAIR),
+                in_=pairs[:].rearrange("p u m -> p (u m)").bitcast(BF16).rearrange("p (u m c) -> p u c m", u=2, c=PAIR),
+            )
+
         total = keep.tile([P, PACK], F32)
         nc.vector.tensor_reduce(out=total[:], in_=powers[:], axis=X, op=ALU.add)
         inv_total = keep.tile([P, PACK], F32)
@@ -80,35 +106,11 @@ def tile_dynamix_pb_kernel(tc, z, mlp_out, t2, A, W, h, grad_out, out):
             op=ALU.mult,
         )
 
-        g_planes = keep.tile([P, PACK, ROWS], BF16)
-        for u in range(2):
-            g_turned = turned.tile([P, ROWS], F32, tag="turned")
-            for i in range(ROW_TILES):
-                nc.tensor.transpose(
-                    g_turned[:, i * P : (i + 1) * P],
-                    g_rows[:, i, :].bitcast(F32)[:, u * P : (u + 1) * P],
-                    identity[:],
-                )
-            copy = nc.vector.tensor_copy if u == 0 else nc.scalar.copy
-            copy(
-                out=g_planes[:, PAIR * u : PAIR * (u + 1), :],
-                in_=g_turned[:].bitcast(BF16).rearrange("p (m c) -> p c m", c=PAIR),
-            )
-
         z_pairs = keep.tile([P, COLS, 2], F32, align_bytes=64)
-        half_cols = COLS // 2
         for half in range(2):
-            z_turned = turned.tile([P, 2, half_cols], F32, tag="turned")
-            for u in range(2):
-                for j in range(2):
-                    nc.tensor.transpose(
-                        z_turned[:, u, j * P : (j + 1) * P],
-                        z_rows[:, 2 * half + j, :].bitcast(F32)[:, u * P : (u + 1) * P],
-                        identity[:],
-                    )
+            pairs = turn(z_rows, half)
             nc.scalar.copy(
-                out=z_pairs[:, half * half_cols : (half + 1) * half_cols, :],
-                in_=z_turned[:].rearrange("p u k -> p k u"),
+                out=z_pairs[:, half * HALF : (half + 1) * HALF, :], in_=pairs[:].rearrange("p u k -> p k u")
             )
         z_grouped = z_pairs[:].rearrange("p k u -> p (k u)").bitcast(BF16)
         z_codes = keep.tile([P, COLS], U32, align_bytes=64)
@@ -122,10 +124,13 @@ def tile_dynamix_pb_kernel(tc, z, mlp_out, t2, A, W, h, grad_out, out):
         def weigh(e):
             planes = work.tile([P, PACK, ROWS], BF16, tag="planes")
             for t in range(PACK):
-                nc.vector.tensor_scalar(
-                    out=planes[:, t, :], in0=g_planes[:, t, :], scalar1=gate[:, t, e : e + 1], scalar2=None,
-                    op0=ALU.mult,
-                )
+                weight = gate[:, t, e : e + 1]
+                if e == 1:
+                    nc.scalar.activation(out=planes[:, t, :], in_=g_planes[:, t, :], func=ACT.Copy, scale=weight)
+                else:
+                    nc.vector.tensor_scalar(
+                        out=planes[:, t, :], in0=g_planes[:, t, :], scalar1=weight, scalar2=None, op0=ALU.mult
+                    )
             return planes
 
         def group(planes):
@@ -142,23 +147,26 @@ def tile_dynamix_pb_kernel(tc, z, mlp_out, t2, A, W, h, grad_out, out):
             nc.vector.quantize_mx(
                 out=codes[:].bitcast(E5M2_X4), scales=scales[:], in_=grouped[:].rearrange("p m t -> p (m t)")
             )
+            last = e == EXPERTS - 1
+            banks_per_store = 1 if e == 0 or last else BANKS_PER_STORE
             out_rows = out[e].rearrange("(r i) k -> r i k", i=ROW_TILES)
-            for first in range(0, ROW_TILES, BANKS_PER_STORE):
-                result = stage.tile([P, BANKS_PER_STORE, COLS], F32, tag="result")
-                for j in range(BANKS_PER_STORE):
-                    rows = slice((first + j) * P, (first + j + 1) * P)
+            for first in range(0, ROW_TILES, banks_per_store):
+                result = stage.tile([P, banks_per_store, COLS], F32, tag="result")
+                for j in range(banks_per_store):
+                    i = first + j
                     acc = sums.tile([P, COLS], F32, tag="acc")
                     nc.tensor.matmul_mx(
                         out=acc[:],
-                        lhsT=codes[:, rows].bitcast(E5M2_X4),
-                        lhsT_scale=scales[:, rows],
+                        lhsT=codes[:, i * P : (i + 1) * P].bitcast(E5M2_X4),
+                        lhsT_scale=scales[:, i * P : (i + 1) * P],
                         rhs=z_codes[:].bitcast(E4M3_X4),
                         rhs_scale=z_scales[:],
                         start=True,
                         stop=True,
                     )
-                    nc.scalar.copy(out=result[:, j, :], in_=acc[:])
-                nc.sync.dma_start(out=out_rows[:, first : first + BANKS_PER_STORE, :], in_=result[:])
+                    empty = nc.vector.tensor_copy if last and i % 2 == 1 else nc.scalar.copy
+                    empty(out=result[:, j, :], in_=acc[:])
+                nc.sync.dma_start(out=out_rows[:, first : first + banks_per_store, :], in_=result[:])
 
         grouped_now = group(weigh(0))
         planes_next = weigh(1)

@@ -36,8 +36,7 @@ def tile_dynamix_pb_kernel(tc, z, mlp_out, t2, A, W, h, grad_out, out):
         keep = ctx.enter_context(tc.tile_pool(name="keep", bufs=1))
         work = ctx.enter_context(tc.tile_pool(name="work", bufs=3))
         stage = ctx.enter_context(tc.tile_pool(name="stage", bufs=8))
-        turned = ctx.enter_context(tc.psum_pool(name="turned", bufs=2))
-        sums = ctx.enter_context(tc.psum_pool(name="sums", bufs=6))
+        banks = ctx.enter_context(tc.psum_pool(name="banks", bufs=8))
 
         logits = keep.tile([P, PACK, EXPERTS], BF16)
         nc.sync.dma_start(
@@ -57,60 +56,61 @@ def tile_dynamix_pb_kernel(tc, z, mlp_out, t2, A, W, h, grad_out, out):
         identity = keep.tile([P, P], F32)
         make_identity(nc, identity[:])
 
-        def turn(rows, half):
-            pairs = turned.tile([P, 2, HALF], F32, tag="pairs")
-            for u in range(2):
-                for j in range(2):
-                    nc.tensor.transpose(
-                        pairs[:, u, j * P : (j + 1) * P],
-                        rows[:, 2 * half + j, :].bitcast(F32)[:, u * P : (u + 1) * P],
-                        identity[:],
-                    )
-            return pairs
+        def turn(target, rows, half, u):
+            for j in range(2):
+                nc.tensor.transpose(
+                    target[:, j * P : (j + 1) * P],
+                    rows[:, 2 * half + j, :].bitcast(F32)[:, u * P : (u + 1) * P],
+                    identity[:],
+                )
 
+        lowest = keep.tile([P, PACK], F32)
+        nc.vector.tensor_reduce(out=lowest[:], in_=logits[:], axis=X, op=ALU.min)
         inv_t = keep.tile([P, 1], F32)
         nc.vector.reciprocal(out=inv_t[:], in_=temperature[:])
-        scores = keep.tile([P, PACK, EXPERTS], F32)
-        nc.vector.tensor_scalar(
-            out=scores[:], in0=logits[:], scalar1=inv_t[:, 0:1], scalar2=-1.0, op0=ALU.mult, op1=ALU.mult
-        )
-        top = keep.tile([P, PACK], F32)
-        nc.vector.tensor_reduce(out=top[:], in_=scores[:], axis=X, op=ALU.max)
+        below = keep.tile([P, PACK, EXPERTS], F32)
         nc.vector.tensor_tensor(
-            out=scores[:],
-            in0=scores[:],
-            in1=top[:].unsqueeze(2).to_broadcast([P, PACK, EXPERTS]),
+            out=below[:],
+            in0=lowest[:].unsqueeze(2).to_broadcast([P, PACK, EXPERTS]),
+            in1=logits[:],
             op=ALU.subtract,
         )
         powers = keep.tile([P, PACK, EXPERTS], F32)
-        nc.scalar.activation(out=powers[:], in_=scores[:], func=ACT.Exp)
+        nc.scalar.activation(out=powers[:], in_=below[:], func=ACT.Exp, scale=inv_t[:, 0:1])
 
         g_planes = keep.tile([P, PACK, ROWS], BF16)
         for half in range(2):
-            pairs = turn(g_rows, half)
             copy = nc.vector.tensor_copy if half == 0 else nc.scalar.copy
-            copy(
-                out=g_planes[:, :, half * HALF : (half + 1) * HALF].rearrange("p (u c) m -> p u c m", c=PAIR),
-                in_=pairs[:].rearrange("p u m -> p (u m)").bitcast(BF16).rearrange("p (u m c) -> p u c m", u=2, c=PAIR),
-            )
+            for u in range(2):
+                pairs = banks.tile([P, COLS], F32, tag="bank")
+                turn(pairs[:, 0:HALF], g_rows, half, u)
+                copy(
+                    out=g_planes[:, PAIR * u : PAIR * (u + 1), half * HALF : (half + 1) * HALF],
+                    in_=pairs[:, 0:HALF].bitcast(BF16).rearrange("p (m c) -> p c m", c=PAIR),
+                )
 
         total = keep.tile([P, PACK], F32)
         nc.vector.tensor_reduce(out=total[:], in_=powers[:], axis=X, op=ALU.add)
         inv_total = keep.tile([P, PACK], F32)
         nc.vector.reciprocal(out=inv_total[:], in_=total[:])
         gate = keep.tile([P, PACK, EXPERTS], F32)
-        nc.vector.tensor_tensor(
-            out=gate[:],
-            in0=powers[:],
-            in1=inv_total[:].unsqueeze(2).to_broadcast([P, PACK, EXPERTS]),
-            op=ALU.mult,
-        )
+
+        def divide_gate():
+            nc.vector.tensor_tensor(
+                out=gate[:],
+                in0=powers[:],
+                in1=inv_total[:].unsqueeze(2).to_broadcast([P, PACK, EXPERTS]),
+                op=ALU.mult,
+            )
 
         z_pairs = keep.tile([P, COLS, 2], F32, align_bytes=64)
         for half in range(2):
-            pairs = turn(z_rows, half)
+            pairs = banks.tile([P, COLS], F32, tag="bank")
+            for u in range(2):
+                turn(pairs[:, u * HALF : (u + 1) * HALF], z_rows, half, u)
             nc.scalar.copy(
-                out=z_pairs[:, half * HALF : (half + 1) * HALF, :], in_=pairs[:].rearrange("p u k -> p k u")
+                out=z_pairs[:, half * HALF : (half + 1) * HALF, :],
+                in_=pairs[:].rearrange("p (u k) -> p k u", u=2),
             )
         z_grouped = z_pairs[:].rearrange("p k u -> p (k u)").bitcast(BF16)
         z_codes = keep.tile([P, COLS], U32, align_bytes=64)
@@ -125,7 +125,16 @@ def tile_dynamix_pb_kernel(tc, z, mlp_out, t2, A, W, h, grad_out, out):
             planes = work.tile([P, PACK, ROWS], BF16, tag="planes")
             for t in range(PACK):
                 weight = gate[:, t, e : e + 1]
-                if e == 1:
+                if e == 0:
+                    nc.vector.tensor_scalar(
+                        out=planes[:, t, :],
+                        in0=g_planes[:, t, :],
+                        scalar1=powers[:, t, 0:1],
+                        scalar2=inv_total[:, t : t + 1],
+                        op0=ALU.mult,
+                        op1=ALU.mult,
+                    )
+                elif e == 1:
                     nc.scalar.activation(out=planes[:, t, :], in_=g_planes[:, t, :], func=ACT.Copy, scale=weight)
                 else:
                     nc.vector.tensor_scalar(
@@ -154,7 +163,7 @@ def tile_dynamix_pb_kernel(tc, z, mlp_out, t2, A, W, h, grad_out, out):
                 result = stage.tile([P, banks_per_store, COLS], F32, tag="result")
                 for j in range(banks_per_store):
                     i = first + j
-                    acc = sums.tile([P, COLS], F32, tag="acc")
+                    acc = banks.tile([P, COLS], F32, tag="bank")
                     nc.tensor.matmul_mx(
                         out=acc[:],
                         lhsT=codes[:, i * P : (i + 1) * P].bitcast(E5M2_X4),
@@ -168,7 +177,9 @@ def tile_dynamix_pb_kernel(tc, z, mlp_out, t2, A, W, h, grad_out, out):
                     empty(out=result[:, j, :], in_=acc[:])
                 nc.sync.dma_start(out=out_rows[:, first : first + banks_per_store, :], in_=result[:])
 
-        grouped_now = group(weigh(0))
+        planes_now = weigh(0)
+        divide_gate()
+        grouped_now = group(planes_now)
         planes_next = weigh(1)
         quantise_z()
         for e in range(EXPERTS):

@@ -25,6 +25,7 @@ ROW_TILES = ROWS // P
 COL_TILES = COLS // P
 HALF = 2 * P
 BANKS_PER_STORE = 2
+WARM_UPS = 5
 
 FLOPS = 2 * EXPERTS * ROWS * COLS * TOKENS
 BYTES = 2 * (ROWS * TOKENS + COLS * TOKENS + TOKENS * EXPERTS + 1) + 4 * EXPERTS * ROWS * COLS
@@ -37,6 +38,12 @@ def tile_dynamix_pb_kernel(tc, z, mlp_out, t2, A, W, h, grad_out, out):
         work = ctx.enter_context(tc.tile_pool(name="work", bufs=3))
         stage = ctx.enter_context(tc.tile_pool(name="stage", bufs=8))
         banks = ctx.enter_context(tc.psum_pool(name="banks", bufs=8))
+
+        zeros = keep.tile([P, COLS], BF16)
+        nc.vector.memset(zeros[:], 0.0)
+        for n in range(WARM_UPS):
+            unused = banks.tile([P, COLS], F32, tag="bank")
+            nc.tensor.matmul(out=unused[:], lhsT=zeros[:, 0:P], rhs=zeros[:], start=True, stop=True)
 
         logits = keep.tile([P, PACK, EXPERTS], BF16)
         nc.sync.dma_start(

@@ -25,7 +25,7 @@ ROW_TILES = ROWS // P
 COL_TILES = COLS // P
 HALF = 2 * P
 BANKS_PER_STORE = 2
-WARM_UPS = 5
+WARM_UPS = 20
 
 FLOPS = 2 * EXPERTS * ROWS * COLS * TOKENS
 BYTES = 2 * (ROWS * TOKENS + COLS * TOKENS + TOKENS * EXPERTS + 1) + 4 * EXPERTS * ROWS * COLS
@@ -39,11 +39,11 @@ def tile_dynamix_pb_kernel(tc, z, mlp_out, t2, A, W, h, grad_out, out):
         stage = ctx.enter_context(tc.tile_pool(name="stage", bufs=8))
         banks = ctx.enter_context(tc.psum_pool(name="banks", bufs=8))
 
-        zeros = keep.tile([P, COLS], BF16)
+        zeros = keep.tile([P, P], BF16)
         nc.vector.memset(zeros[:], 0.0)
+        unused = banks.tile([P, COLS], F32, tag="bank")
         for n in range(WARM_UPS):
-            unused = banks.tile([P, COLS], F32, tag="bank")
-            nc.tensor.matmul(out=unused[:], lhsT=zeros[:, 0:P], rhs=zeros[:], start=True, stop=True)
+            nc.tensor.matmul(out=unused[:, 0:P], lhsT=zeros[:], rhs=zeros[:], start=True, stop=True)
 
         logits = keep.tile([P, PACK, EXPERTS], BF16)
         nc.sync.dma_start(

@@ -149,24 +149,24 @@ def tile_dynamix_pb_kernel(tc, z, mlp_out, t2, A, W, h, grad_out, out):
                     )
             return planes
 
-        def group(planes):
-            grouped = work.tile([P, ROWS, PACK], BF16, tag="grouped", align_bytes=64)
+        def group(planes, start=0, width=ROWS):
+            grouped = work.tile([P, width, PACK], BF16, tag="grouped", align_bytes=64)
             nc.vector.tensor_copy(
                 out=grouped[:].rearrange("p (c n) t -> p c t n", n=4),
-                in_=planes[:].rearrange("p t (c n) -> p c t n", n=4),
+                in_=planes[:, :, start : start + width].rearrange("p t (c n) -> p c t n", n=4),
             )
             return grouped
 
-        def multiply(e, grouped):
-            codes = work.tile([P, ROWS], U32, tag="codes", align_bytes=64)
-            scales = work.tile([P, ROWS], U8, tag="scales", align_bytes=64)
+        def multiply(e, grouped, start=0, width=ROWS):
+            codes = work.tile([P, width], U32, tag="codes", align_bytes=64)
+            scales = work.tile([P, width], U8, tag="scales", align_bytes=64)
             nc.vector.quantize_mx(
                 out=codes[:].bitcast(E5M2_X4), scales=scales[:], in_=grouped[:].rearrange("p m t -> p (m t)")
             )
             last = e == EXPERTS - 1
             banks_per_store = 1 if e == 0 or last else BANKS_PER_STORE
             out_rows = out[e].rearrange("(r i) k -> r i k", i=ROW_TILES)
-            for first in range(0, ROW_TILES, banks_per_store):
+            for first in range(0, width // P, banks_per_store):
                 result = stage.tile([P, banks_per_store, COLS], F32, tag="result")
                 for j in range(banks_per_store):
                     i = first + j
@@ -182,16 +182,24 @@ def tile_dynamix_pb_kernel(tc, z, mlp_out, t2, A, W, h, grad_out, out):
                     )
                     empty = nc.vector.tensor_copy if last and i % 2 == 1 else nc.scalar.copy
                     empty(out=result[:, j, :], in_=acc[:])
-                nc.sync.dma_start(out=out_rows[:, first : first + banks_per_store, :], in_=result[:])
+                row_tile = start // P + first
+                nc.sync.dma_start(out=out_rows[:, row_tile : row_tile + banks_per_store, :], in_=result[:])
 
         planes_now = weigh(0)
         divide_gate()
-        grouped_now = group(planes_now)
+        grouped_now = group(planes_now, 0, HALF)
         planes_next = weigh(1)
         quantise_z()
-        for e in range(EXPERTS):
-            multiply(e, grouped_now)
-            if e + 1 < EXPERTS:
-                grouped_now = group(planes_next)
+        multiply(0, grouped_now, 0, HALF)
+        grouped_now = group(planes_now, HALF, HALF)
+        for e in range(EXPERTS - 1):
+            if e == 0:
+                multiply(0, grouped_now, HALF, HALF)
+            else:
+                multiply(e, grouped_now)
             if e + 2 < EXPERTS:
+                grouped_now = group(planes_next)
                 planes_next = weigh(e + 2)
+        halves = [group(planes_next, start, HALF) for start in (0, HALF)]
+        for start, grouped_now in zip((0, HALF), halves):
+            multiply(EXPERTS - 1, grouped_now, start, HALF)

from contextlib import ExitStack

import concourse.mybir as mybir
from concourse.masks import make_identity

BF16 = mybir.dt.bfloat16
F32 = mybir.dt.float32
U32 = mybir.dt.uint32
U8 = mybir.dt.uint8
E5M2_X4 = mybir.dt.float8_e5m2_x4
E4M3_X4 = mybir.dt.float8_e4m3fn_x4
ALU = mybir.AluOpType
X = mybir.AxisListType.X
ACT = mybir.ActivationFunctionType

P = 128
PACK = 4
PAIR = 2
TOKENS = P * PACK
EXPERTS = 16
ROWS = 512
COLS = 512
RELU_ROWS = 32
ROW_TILES = ROWS // P
COL_TILES = COLS // P
HALF = 2 * P
BANKS_PER_STORE = 2
WARM_UPS = 20

FLOPS = 2 * EXPERTS * ROWS * COLS * TOKENS
BYTES = 2 * (ROWS * TOKENS + COLS * TOKENS + TOKENS * EXPERTS + 1) + 4 * EXPERTS * ROWS * COLS


def tile_dynamix_pb_kernel(tc, z, mlp_out, t2, A, W, h, grad_out, out):
    nc = tc.nc
    with ExitStack() as ctx:
        keep = ctx.enter_context(tc.tile_pool(name="keep", bufs=1))
        work = ctx.enter_context(tc.tile_pool(name="work", bufs=3))
        stage = ctx.enter_context(tc.tile_pool(name="stage", bufs=8))
        banks = ctx.enter_context(tc.psum_pool(name="banks", bufs=8))

        zeros = keep.tile([P, P], BF16)
        nc.vector.memset(zeros[:], 0.0)
        unused = banks.tile([P, COLS], F32, tag="bank")
        for n in range(WARM_UPS):
            nc.tensor.matmul(out=unused[:, 0:P], lhsT=zeros[:], rhs=zeros[:], start=True, stop=True)

        logits = keep.tile([P, PACK, EXPERTS], BF16)
        nc.sync.dma_start(
            out=logits[:].rearrange("p (u c) e -> p u c e", c=PAIR),
            in_=mlp_out.rearrange("(u p c) e -> p u c e", p=P, c=PAIR),
        )
        temperature = keep.tile([P, 1], BF16)
        nc.sync.dma_start(out=temperature[:], in_=t2.partition_broadcast(P))
        g_rows = keep.tile([P, ROW_TILES, TOKENS], BF16)
        g_source = grad_out.rearrange("(r i) b -> r i b", i=ROW_TILES)
        z_rows = keep.tile([P, COL_TILES, TOKENS], BF16)
        z_source = z.rearrange("(i r) b -> r i b", r=P)
        for rows, source in ((g_rows, g_source), (z_rows, z_source)):
            for half in range(2):
                nc.sync.dma_start(out=rows[:, 2 * half : 2 * half + 2, :], in_=source[:, 2 * half : 2 * half + 2, :])

        identity = keep.tile([P, P], F32)
        make_identity(nc, identity[:])

        def turn(target, rows, half, u):
            for j in range(2):
                nc.tensor.transpose(
                    target[:, j * P : (j + 1) * P],
                    rows[:, 2 * half + j, :].bitcast(F32)[:, u * P : (u + 1) * P],
                    identity[:],
                )

        lowest = keep.tile([P, PACK], F32)
        nc.vector.tensor_reduce(out=lowest[:], in_=logits[:], axis=X, op=ALU.min)
        inv_t = keep.tile([P, 1], F32)
        nc.vector.reciprocal(out=inv_t[:], in_=temperature[:])
        below = keep.tile([P, PACK, EXPERTS], F32)
        nc.vector.tensor_tensor(
            out=below[:],
            in0=lowest[:].unsqueeze(2).to_broadcast([P, PACK, EXPERTS]),
            in1=logits[:],
            op=ALU.subtract,
        )
        powers = keep.tile([P, PACK, EXPERTS], F32)
        nc.scalar.activation(out=powers[:], in_=below[:], func=ACT.Exp, scale=inv_t[:, 0:1])

        g_planes = keep.tile([P, PACK, ROWS], BF16)
        for half in range(2):
            copy = nc.vector.tensor_copy if half == 0 else nc.scalar.copy
            for u in range(2):
                pairs = banks.tile([P, COLS], F32, tag="bank")
                turn(pairs[:, 0:HALF], g_rows, half, u)
                copy(
                    out=g_planes[:, PAIR * u : PAIR * (u + 1), half * HALF : (half + 1) * HALF],
                    in_=pairs[:, 0:HALF].bitcast(BF16).rearrange("p (m c) -> p c m", c=PAIR),
                )

        total = keep.tile([P, PACK], F32)
        nc.vector.tensor_reduce(out=total[:], in_=powers[:], axis=X, op=ALU.add)
        inv_total = keep.tile([P, PACK], F32)
        nc.vector.reciprocal(out=inv_total[:], in_=total[:])
        gate = keep.tile([P, PACK, EXPERTS], F32)

        def divide_gate():
            nc.vector.tensor_tensor(
                out=gate[:],
                in0=powers[:],
                in1=inv_total[:].unsqueeze(2).to_broadcast([P, PACK, EXPERTS]),
                op=ALU.mult,
            )

        z_pairs = keep.tile([P, COLS, 2], F32, align_bytes=64)
        for half in range(2):
            pairs = banks.tile([P, COLS], F32, tag="bank")
            for u in range(2):
                turn(pairs[:, u * HALF : (u + 1) * HALF], z_rows, half, u)
            nc.scalar.copy(
                out=z_pairs[:, half * HALF : (half + 1) * HALF, :],
                in_=pairs[:].rearrange("p (u k) -> p k u", u=2),
            )
        z_grouped = z_pairs[:].rearrange("p k u -> p (k u)").bitcast(BF16)
        z_codes = keep.tile([P, COLS], U32, align_bytes=64)
        z_scales = keep.tile([P, COLS], U8, align_bytes=64)

        def quantise_z():
            relu_part = z_grouped[:, (COLS - RELU_ROWS) * PACK :]
            nc.vector.tensor_scalar_max(out=relu_part, in0=relu_part, scalar1=0.0)
            nc.vector.quantize_mx(out=z_codes[:].bitcast(E4M3_X4), scales=z_scales[:], in_=z_grouped)

        def weigh(e):
            planes = work.tile([P, PACK, ROWS], BF16, tag="planes")
            for t in range(PACK):
                weight = gate[:, t, e : e + 1]
                if e == 0:
                    nc.vector.tensor_scalar(
                        out=planes[:, t, :],
                        in0=g_planes[:, t, :],
                        scalar1=powers[:, t, 0:1],
                        scalar2=inv_total[:, t : t + 1],
                        op0=ALU.mult,
                        op1=ALU.mult,
                    )
                elif e == 1:
                    nc.scalar.activation(out=planes[:, t, :], in_=g_planes[:, t, :], func=ACT.Copy, scale=weight)
                else:
                    nc.vector.tensor_scalar(
                        out=planes[:, t, :], in0=g_planes[:, t, :], scalar1=weight, scalar2=None, op0=ALU.mult
                    )
            return planes

        def group(planes, start=0, width=ROWS):
            grouped = work.tile([P, width, PACK], BF16, tag="grouped", align_bytes=64)
            nc.vector.tensor_copy(
                out=grouped[:].rearrange("p (c n) t -> p c t n", n=4),
                in_=planes[:, :, start : start + width].rearrange("p t (c n) -> p c t n", n=4),
            )
            return grouped

        def multiply(e, grouped, start=0, width=ROWS):
            codes = work.tile([P, width], U32, tag="codes", align_bytes=64)
            scales = work.tile([P, width], U8, tag="scales", align_bytes=64)
            nc.vector.quantize_mx(
                out=codes[:].bitcast(E5M2_X4), scales=scales[:], in_=grouped[:].rearrange("p m t -> p (m t)")
            )
            last = e == EXPERTS - 1
            banks_per_store = 1 if e == 0 or last else BANKS_PER_STORE
            out_rows = out[e].rearrange("(r i) k -> r i k", i=ROW_TILES)
            for first in range(0, width // P, banks_per_store):
                result = stage.tile([P, banks_per_store, COLS], F32, tag="result")
                for j in range(banks_per_store):
                    i = first + j
                    acc = banks.tile([P, COLS], F32, tag="bank")
                    nc.tensor.matmul_mx(
                        out=acc[:],
                        lhsT=codes[:, i * P : (i + 1) * P].bitcast(E5M2_X4),
                        lhsT_scale=scales[:, i * P : (i + 1) * P],
                        rhs=z_codes[:].bitcast(E4M3_X4),
                        rhs_scale=z_scales[:],
                        start=True,
                        stop=True,
                    )
                    empty = nc.vector.tensor_copy if last and i % 2 == 1 else nc.scalar.copy
                    empty(out=result[:, j, :], in_=acc[:])
                row_tile = start // P + first
                nc.sync.dma_start(out=out_rows[:, row_tile : row_tile + banks_per_store, :], in_=result[:])

        planes_now = weigh(0)
        divide_gate()
        grouped_now = group(planes_now, 0, HALF)
        planes_next = weigh(1)
        quantise_z()
        multiply(0, grouped_now, 0, HALF)
        grouped_now = group(planes_now, HALF, HALF)
        for e in range(EXPERTS - 1):
            if e == 0:
                multiply(0, grouped_now, HALF, HALF)
            else:
                multiply(e, grouped_now)
            if e + 2 < EXPERTS:
                grouped_now = group(planes_next)
                planes_next = weigh(e + 2)
        halves = [group(planes_next, start, HALF) for start in (0, HALF)]
        for start, grouped_now in zip((0, HALF), halves):
            multiply(EXPERTS - 1, grouped_now, start, HALF)
